import numpy as np
import ml_dtypes

BF16 = ml_dtypes.bfloat16


def bf(x):
    return np.asarray(x, np.float32).astype(BF16)


def f32(x):
    return np.asarray(x, np.float32)


def f64(x):
    return np.asarray(x).astype(np.float64)


def striped(idx):
    return np.tile(idx.reshape(-1, 16).T, (8, 1))


C, S, L, N = 256, 2048, 512, 1024


def setup_inputs():
    return {"emb": f32(np.random.standard_normal((C, S))), "pos": f32(np.random.standard_normal((C, L))), "offs": striped(np.random.permutation(np.tile(np.arange(S), 2))[:N])}


def reference(emb, pos, offs):
    idx = offs[:16].T.reshape(-1)
    return f64(emb)[:, idx] + np.tile(f64(pos), (1, N // L))

@@ -1,0 +1,28 @@
+import concourse.mybir as mybir
+
+F32 = mybir.dt.float32
+U16 = mybir.dt.uint16
+ADD = mybir.AluOpType.add
+
+P = 128
+C, S, L, N = 256, 2048, 512, 1024
+
+
+def tile_edtransformer_kernel(tc, emb, pos, offs, out):
+    nc = tc.nc
+    with tc.tile_pool(name="held", bufs=1) as held:
+        offsets = held.tile([P, N // 16], U16, name="offsets")
+        nc.sync.dma_start(offsets[:], offs)
+
+        for b in range(C // P):
+            rows = slice(b * P, (b + 1) * P)
+            table = held.tile([P, S], F32, name=f"table{b}")
+            nc.sync.dma_start(table[:], emb[rows, :])
+            position = held.tile([P, L], F32, name=f"position{b}")
+            nc.sync.dma_start(position[:], pos[rows, :])
+
+            for q in range(N // L):
+                summed = held.tile([P, L], F32, name=f"summed{b}_{q}")
+                picked = table[:].indirect(offsets[:, q * (L // 16) : (q + 1) * (L // 16)])
+                nc.vector.tensor_tensor(summed[:], picked, position[:], ADD)
+                nc.scalar.dma_start(out[rows, q * L : (q + 1) * L], summed[:])

@@ -6,6 +6,7 @@ ADD = mybir.AluOpType.add
 
 P = 128
 C, S, L, N = 256, 2048, 512, 1024
+PIECE = 256
 
 
 def tile_edtransformer_kernel(tc, emb, pos, offs, out):
@@ -21,8 +22,9 @@ def tile_edtransformer_kernel(tc, emb, pos, offs, out):
             position = held.tile([P, L], F32, name=f"position{b}")
             nc.sync.dma_start(position[:], pos[rows, :])
 
-            for q in range(N // L):
-                summed = held.tile([P, L], F32, name=f"summed{b}_{q}")
-                picked = table[:].indirect(offsets[:, q * (L // 16) : (q + 1) * (L // 16)])
-                nc.vector.tensor_tensor(summed[:], picked, position[:], ADD)
-                nc.scalar.dma_start(out[rows, q * L : (q + 1) * L], summed[:])
+            for first in range(0, N, PIECE):
+                summed = held.tile([P, PIECE], F32, name=f"summed{b}_{first}")
+                picked = table[:].indirect(offsets[:, first // 16 : (first + PIECE) // 16])
+                at = first % L
+                nc.vector.tensor_tensor(summed[:], picked, position[:, at : at + PIECE], ADD)
+                nc.scalar.dma_start(out[rows, first : first + PIECE], summed[:])

@@ -18,7 +18,7 @@ def tile_edtransformer_kernel(tc, emb, pos, offs, out):
         for b in range(C // P):
             rows = slice(b * P, (b + 1) * P)
             table = held.tile([P, S], F32, name=f"table{b}")
-            nc.sync.dma_start(table[:], emb[rows, :])
+            nc.scalar.dma_start(table[:], emb[rows, :])
             position = held.tile([P, L], F32, name=f"position{b}")
             nc.sync.dma_start(position[:], pos[rows, :])
 
@@ -27,4 +27,4 @@ def tile_edtransformer_kernel(tc, emb, pos, offs, out):
                 picked = table[:].indirect(offsets[:, first // 16 : (first + PIECE) // 16])
                 at = first % L
                 nc.vector.tensor_tensor(summed[:], picked, position[:, at : at + PIECE], ADD)
-                nc.scalar.dma_start(out[rows, first : first + PIECE], summed[:])
+                nc.sync.dma_start(out[rows, first : first + PIECE], summed[:])

@@ -6,7 +6,7 @@ ADD = mybir.AluOpType.add
 
 P = 128
 C, S, L, N = 256, 2048, 512, 1024
-PIECE = 256
+PIECE = L // 2
 
 
 def tile_edtransformer_kernel(tc, emb, pos, offs, out):
@@ -18,13 +18,14 @@ def tile_edtransformer_kernel(tc, emb, pos, offs, out):
         for b in range(C // P):
             rows = slice(b * P, (b + 1) * P)
             table = held.tile([P, S], F32, name=f"table{b}")
-            nc.scalar.dma_start(table[:], emb[rows, :])
-            position = held.tile([P, L], F32, name=f"position{b}")
-            nc.sync.dma_start(position[:], pos[rows, :])
+            nc.sync.dma_start(table[:], emb[rows, :])
 
-            for first in range(0, N, PIECE):
-                summed = held.tile([P, PIECE], F32, name=f"summed{b}_{first}")
-                picked = table[:].indirect(offsets[:, first // 16 : (first + PIECE) // 16])
-                at = first % L
-                nc.vector.tensor_tensor(summed[:], picked, position[:, at : at + PIECE], ADD)
-                nc.sync.dma_start(out[rows, first : first + PIECE], summed[:])
+            for at in range(0, L, PIECE):
+                position = held.tile([P, PIECE], F32, name=f"position{b}_{at}")
+                nc.sync.dma_start(position[:], pos[rows, at : at + PIECE])
+
+                for first in range(at, N, L):
+                    summed = held.tile([P, PIECE], F32, name=f"summed{b}_{first}")
+                    picked = table[:].indirect(offsets[:, first // 16 : (first + PIECE) // 16])
+                    nc.vector.tensor_tensor(summed[:], picked, position[:], ADD)
+                    nc.scalar.dma_start(out[rows, first : first + PIECE], summed[:])

@@ -6,7 +6,8 @@ ADD = mybir.AluOpType.add
 
 P = 128
 C, S, L, N = 256, 2048, 512, 1024
-PIECE = L // 2
+EDGE = 128
+CUTS = (0, EDGE, L, N - EDGE, N)
 
 
 def tile_edtransformer_kernel(tc, emb, pos, offs, out):
@@ -20,12 +21,12 @@ def tile_edtransformer_kernel(tc, emb, pos, offs, out):
             table = held.tile([P, S], F32, name=f"table{b}")
             nc.sync.dma_start(table[:], emb[rows, :])
 
-            for at in range(0, L, PIECE):
-                position = held.tile([P, PIECE], F32, name=f"position{b}_{at}")
-                nc.sync.dma_start(position[:], pos[rows, at : at + PIECE])
+            position = held.tile([P, L], F32, name=f"position{b}")
+            nc.sync.dma_start(position[:, :EDGE], pos[rows, :EDGE])
+            nc.sync.dma_start(position[:, EDGE:], pos[rows, EDGE:])
 
-                for first in range(at, N, L):
-                    summed = held.tile([P, PIECE], F32, name=f"summed{b}_{first}")
-                    picked = table[:].indirect(offsets[:, first // 16 : (first + PIECE) // 16])
-                    nc.vector.tensor_tensor(summed[:], picked, position[:], ADD)
-                    nc.scalar.dma_start(out[rows, first : first + PIECE], summed[:])
+            for first, end in zip(CUTS[:-1], CUTS[1:]):
+                summed = held.tile([P, end - first], F32, name=f"summed{b}_{first}")
+                picked = table[:].indirect(offsets[:, first // 16 : end // 16])
+                nc.vector.tensor_tensor(summed[:], picked, position[:, first % L : first % L + end - first], ADD)
+                nc.scalar.dma_start(out[rows, first:end], summed[:])

@@ -6,6 +6,7 @@ ADD = mybir.AluOpType.add
 
 P = 128
 C, S, L, N = 256, 2048, 512, 1024
+BLOCKS = C // P
 EDGE = 128
 CUTS = (0, EDGE, L, N - EDGE, N)
 
@@ -16,13 +17,13 @@ def tile_edtransformer_kernel(tc, emb, pos, offs, out):
         offsets = held.tile([P, N // 16], U16, name="offsets")
         nc.sync.dma_start(offsets[:], offs)
 
-        for b in range(C // P):
+        for b in range(BLOCKS):
             rows = slice(b * P, (b + 1) * P)
             table = held.tile([P, S], F32, name=f"table{b}")
-            nc.sync.dma_start(table[:], emb[rows, :])
-
             position = held.tile([P, L], F32, name=f"position{b}")
+
             nc.sync.dma_start(position[:, :EDGE], pos[rows, :EDGE])
+            nc.sync.dma_start(table[:], emb[rows, :])
             nc.sync.dma_start(position[:, EDGE:], pos[rows, EDGE:])
 
             for first, end in zip(CUTS[:-1], CUTS[1:]):

@@ -7,8 +7,9 @@ ADD = mybir.AluOpType.add
 P = 128
 C, S, L, N = 256, 2048, 512, 1024
 BLOCKS = C // P
-EDGE = 128
-CUTS = (0, EDGE, L, N - EDGE, N)
+HEAD = 128
+TAIL = 3 * L // 8
+CUTS = (0, HEAD, L, N - TAIL, N)
 
 
 def tile_edtransformer_kernel(tc, emb, pos, offs, out):
@@ -22,9 +23,9 @@ def tile_edtransformer_kernel(tc, emb, pos, offs, out):
             table = held.tile([P, S], F32, name=f"table{b}")
             position = held.tile([P, L], F32, name=f"position{b}")
 
-            nc.sync.dma_start(position[:, :EDGE], pos[rows, :EDGE])
+            nc.sync.dma_start(position[:, :HEAD], pos[rows, :HEAD])
             nc.sync.dma_start(table[:], emb[rows, :])
-            nc.sync.dma_start(position[:, EDGE:], pos[rows, EDGE:])
+            nc.sync.dma_start(position[:, HEAD:], pos[rows, HEAD:])
 
             for first, end in zip(CUTS[:-1], CUTS[1:]):
                 summed = held.tile([P, end - first], F32, name=f"summed{b}_{first}")

@@ -16,15 +16,16 @@ def tile_edtransformer_kernel(tc, emb, pos, offs, out):
     nc = tc.nc
     with tc.tile_pool(name="held", bufs=1) as held:
         offsets = held.tile([P, N // 16], U16, name="offsets")
-        nc.sync.dma_start(offsets[:], offs)
 
         for b in range(BLOCKS):
             rows = slice(b * P, (b + 1) * P)
             table = held.tile([P, S], F32, name=f"table{b}")
             position = held.tile([P, L], F32, name=f"position{b}")
 
-            nc.sync.dma_start(position[:, :HEAD], pos[rows, :HEAD])
+            nc.scalar.dma_start(position[:, :HEAD], pos[rows, :HEAD])
             nc.sync.dma_start(table[:], emb[rows, :])
+            if b == 0:
+                nc.sync.dma_start(offsets[:], offs)
             nc.sync.dma_start(position[:, HEAD:], pos[rows, HEAD:])
 
             for first, end in zip(CUTS[:-1], CUTS[1:]):

@@ -9,7 +9,8 @@ C, S, L, N = 256, 2048, 512, 1024
 BLOCKS = C // P
 HEAD = 128
 TAIL = 3 * L // 8
-CUTS = (0, HEAD, L, N - TAIL, N)
+CUTS = ((0, HEAD, L, N), (0, HEAD, L, N - TAIL, N))
+MOST = (L // 2, L)
 
 
 def tile_edtransformer_kernel(tc, emb, pos, offs, out):
@@ -22,14 +23,17 @@ def tile_edtransformer_kernel(tc, emb, pos, offs, out):
             table = held.tile([P, S], F32, name=f"table{b}")
             position = held.tile([P, L], F32, name=f"position{b}")
 
-            nc.scalar.dma_start(position[:, :HEAD], pos[rows, :HEAD])
+            heads = (nc.scalar, nc.sync)
+            heads[b].dma_start(position[:, :HEAD], pos[rows, :HEAD])
             nc.sync.dma_start(table[:], emb[rows, :])
             if b == 0:
                 nc.sync.dma_start(offsets[:], offs)
             nc.sync.dma_start(position[:, HEAD:], pos[rows, HEAD:])
 
-            for first, end in zip(CUTS[:-1], CUTS[1:]):
+            for first, end in zip(CUTS[b][:-1], CUTS[b][1:]):
                 summed = held.tile([P, end - first], F32, name=f"summed{b}_{first}")
                 picked = table[:].indirect(offsets[:, first // 16 : end // 16])
                 nc.vector.tensor_tensor(summed[:], picked, position[:, first % L : first % L + end - first], ADD)
-                nc.scalar.dma_start(out[rows, first:end], summed[:])
+                for at in range(first, end, MOST[b]):
+                    stop = min(at + MOST[b], end)
+                    nc.scalar.dma_start(out[rows, at:stop], summed[:, at - first : stop - first])

@@ -8,9 +8,9 @@ P = 128
 C, S, L, N = 256, 2048, 512, 1024
 BLOCKS = C // P
 HEAD = 128
-TAIL = 3 * L // 8
-CUTS = ((0, HEAD, L, N), (0, HEAD, L, N - TAIL, N))
-MOST = (L // 2, L)
+TAIL = L // 4
+CUTS = ((0, HEAD, L, N), (0, HEAD, L, N - 2 * TAIL, N - TAIL, N))
+MOST = 3 * L // 4
 
 
 def tile_edtransformer_kernel(tc, emb, pos, offs, out):
@@ -34,6 +34,6 @@ def tile_edtransformer_kernel(tc, emb, pos, offs, out):
                 summed = held.tile([P, end - first], F32, name=f"summed{b}_{first}")
                 picked = table[:].indirect(offsets[:, first // 16 : end // 16])
                 nc.vector.tensor_tensor(summed[:], picked, position[:, first % L : first % L + end - first], ADD)
-                for at in range(first, end, MOST[b]):
-                    stop = min(at + MOST[b], end)
+                for at in range(first, end, MOST):
+                    stop = min(at + MOST, end)
                     nc.scalar.dma_start(out[rows, at:stop], summed[:, at - first : stop - first])

import concourse.mybir as mybir

F32 = mybir.dt.float32
U16 = mybir.dt.uint16
ADD = mybir.AluOpType.add

P = 128
C, S, L, N = 256, 2048, 512, 1024
BLOCKS = C // P
HEAD = 128
TAIL = L // 4
CUTS = ((0, HEAD, L, N), (0, HEAD, L, N - 2 * TAIL, N - TAIL, N))
MOST = 3 * L // 4


def tile_edtransformer_kernel(tc, emb, pos, offs, out):
    nc = tc.nc
    with tc.tile_pool(name="held", bufs=1) as held:
        offsets = held.tile([P, N // 16], U16, name="offsets")

        for b in range(BLOCKS):
            rows = slice(b * P, (b + 1) * P)
            table = held.tile([P, S], F32, name=f"table{b}")
            position = held.tile([P, L], F32, name=f"position{b}")

            heads = (nc.scalar, nc.sync)
            heads[b].dma_start(position[:, :HEAD], pos[rows, :HEAD])
            nc.sync.dma_start(table[:], emb[rows, :])
            if b == 0:
                nc.sync.dma_start(offsets[:], offs)
            nc.sync.dma_start(position[:, HEAD:], pos[rows, HEAD:])

            for first, end in zip(CUTS[b][:-1], CUTS[b][1:]):
                summed = held.tile([P, end - first], F32, name=f"summed{b}_{first}")
                picked = table[:].indirect(offsets[:, first // 16 : end // 16])
                nc.vector.tensor_tensor(summed[:], picked, position[:, first % L : first % L + end - first], ADD)
                for at in range(first, end, MOST):
                    stop = min(at + MOST, end)
                    nc.scalar.dma_start(out[rows, at:stop], summed[:, at - first : stop - first])
